import numpy as np
import ml_dtypes


def mxq(x, axis, fmt="e4m3"):
    dtype, down = {"e4m3": (ml_dtypes.float8_e4m3fn, 7), "e5m2": (ml_dtypes.float8_e5m2, 14)}[fmt]
    v = np.moveaxis(np.asarray(x, np.float32).astype(ml_dtypes.bfloat16).astype(np.float64), axis, -1)
    blocks = v.reshape(v.shape[:-1] + (-1, 32))
    amax = np.abs(blocks).max(-1, keepdims=True)
    byte = np.maximum(np.where(amax > 0, np.frexp(amax)[1] - 1 + 127, 0) - down, 1)
    scale = np.exp2(byte - 127.0)
    codes = (blocks / scale).astype(np.float32).astype(dtype).astype(np.float64)
    return np.moveaxis((codes * scale).reshape(v.shape), -1, axis)


WIDE = False


def mx_kscale(k):
    if not WIDE:
        return np.ones(k)
    levels = np.array([10, -10, 5, -5, 0])
    a = np.random.permutation(np.resize(levels, k // 512 * 4)).reshape(k // 512, 4)
    idx = np.arange(k)
    return np.exp2(a[idx // 512, idx % 128 // 32])


BF16 = ml_dtypes.bfloat16


def bf(x):
    return np.asarray(x, np.float32).astype(BF16)


def f64(x):
    return np.asarray(x).astype(np.float64)


B, G, C, F, NC = 128, 6, 1024, 1024, 4096
HW = G * G
P_GEM = 3.0
EPS_GEM = 1e-6
EPS_NORM = 1e-12


def l2n(v, axis):
    n = np.sqrt(np.sum(v * v, axis=axis, keepdims=True))
    return v / np.maximum(n, EPS_NORM)


def setup_inputs():
    s, t = mx_kscale(F), mx_kscale(C)
    z = np.random.standard_normal((B, HW, F))
    return {"hdn": bf(z / (1.0 + np.exp(-1.702 * z)) * s),
            "fc2_w": bf(np.random.standard_normal((F, C)) * 1.5 / np.sqrt(F) / s[:, None] * t),
            "fc2_b": bf(np.random.standard_normal(C) * 0.3 * t),
            "head_w": bf(np.random.standard_normal((C, NC)) / np.sqrt(C) / t[:, None]),
            "head_b": bf(np.random.standard_normal(NC) * 0.3)}


def reference(hdn, fc2_w, fc2_b, head_w, head_b):
    tok = (mxq(f64(hdn), 2, "e4m3") @ mxq(f64(fc2_w), 0, "e4m3")) + f64(fc2_b)
    g = np.mean(np.maximum(tok, EPS_GEM) ** P_GEM, axis=1) ** (1.0 / P_GEM)
    desc = (mxq(g, 1, "e4m3") @ mxq(f64(head_w), 0, "e4m3")) + f64(head_b)
    return l2n(desc, 1)

@@ -1,0 +1,330 @@
+from contextlib import ExitStack
+
+import concourse.mybir as mybir
+from concourse.masks import make_identity
+
+F32 = mybir.dt.float32
+BF16 = mybir.dt.bfloat16
+U32 = mybir.dt.uint32
+U8 = mybir.dt.uint8
+FP8X4 = mybir.dt.float8_e4m3fn_x4
+ALU = mybir.AluOpType
+ACT = mybir.ActivationFunctionType
+AX = mybir.AxisListType
+
+P = 128
+NB = 128
+NT = 36
+NF = 1024
+NCH = 1024
+NOUT = 4096
+EPS3 = 1e-18
+BIG = 3.0e38
+NSTEP = 18
+NPART = 18
+V_COLS = 320
+
+FLOPS = 2 * NB * NT * NF * NCH + 2 * NB * NCH * NOUT
+
+
+def tile_tokenmudule_pb_kernel(tc, hdn, fc2_w, fc2_b, head_w, head_b, out):
+    nc = tc.nc
+    with ExitStack() as ctx:
+        const = ctx.enter_context(tc.tile_pool(name="const", bufs=1))
+        hr_pool = ctx.enter_context(tc.tile_pool(name="hr", bufs=3))
+        hg_pool = ctx.enter_context(tc.tile_pool(name="hg", bufs=2))
+        hc_pool = ctx.enter_context(tc.tile_pool(name="hc", bufs=3))
+        raw_pool = ctx.enter_context(tc.tile_pool(name="raw", bufs=3))
+        grp_pool = ctx.enter_context(tc.tile_pool(name="grp", bufs=2))
+        s_pool = ctx.enter_context(tc.tile_pool(name="sq", bufs=2))
+        c_pool = ctx.enter_context(tc.tile_pool(name="cube", bufs=3))
+        ps_sum = ctx.enter_context(tc.psum_pool(name="pssum", bufs=1))
+        ps_mm = ctx.enter_context(tc.psum_pool(name="psmm", bufs=4))
+        ps_xt = ctx.enter_context(tc.psum_pool(name="psxt", bufs=2))
+        ctx.enter_context(tc.manual_schedule())
+
+        ident_f = const.tile([P, P], F32)
+        ident_b = const.tile([P, P], BF16)
+        brow = const.tile([P, P], BF16)
+        bias = const.tile([P, 8], F32)
+        one = const.tile([P, 1], F32)
+        dmy = const.tile([P, 1], F32)
+        w_codes = const.tile([P, 2, 2, 512], U32, align_bytes=64)
+        w_scales = const.tile([P, 2, 2, 512], U8, align_bytes=64)
+        hw_codes = const.tile([P, 8, 2, 512], U32, align_bytes=64)
+        hw_scales = const.tile([P, 8, 2, 512], U8, align_bytes=64)
+        hb = const.tile([P, NOUT], BF16)
+        d = const.tile([P, NOUT], F32)
+        junk = const.tile([P, 512], F32)
+        lng = const.tile([P, NCH], F32)
+        gb = const.tile([P, NCH], BF16)
+        g_grp = const.tile([P, 2, P, 4], BF16, align_bytes=64)
+        g_codes = const.tile([P, 2, P], U32, align_bytes=64)
+        g_scales = const.tile([P, 2, P], U8, align_bytes=64)
+        ss = const.tile([P, 8], F32)
+        tot = const.tile([P, 1], F32)
+        nrm = const.tile([P, 1], F32)
+        rinv = const.tile([P, 1], F32)
+        sums = [ps_sum.tile([P, 512], F32, name="sum%d" % i) for i in range(2)]
+
+        hr = {}
+        hg = {}
+        hc = {}
+        hs = {}
+        raw = {}
+        grp = {}
+        xts = {}
+        banks = {}
+        s4 = {}
+        c4 = {}
+
+        def load_h(n):
+            hr[n] = hr_pool.tile([P, 4, NF], BF16, name="hr")
+            nc.sync.dma_start(out=hr[n][:], in_=hdn[:, 4 * n : 4 * n + 4, :])
+
+        def load_chunk(ci):
+            raw[ci] = raw_pool.tile([P, 8, 512], BF16, name="raw")
+            if ci < 2:
+                src = fc2_w[:, 512 * ci : 512 * ci + 512].rearrange("(a p e) c -> e p a c", a=4, p=P, e=2)
+                dst = raw[ci][:].rearrange("p (a e) c -> p a e c", e=2)
+                for e in range(2):
+                    nc.sync.dma_start(out=dst[:, :, e, :], in_=src[e])
+            else:
+                nt = ci - 2
+                nc.sync.dma_start(
+                    out=raw[ci][:],
+                    in_=head_w[:, 512 * nt : 512 * nt + 512].rearrange("(a p) n -> p a n", a=8, p=P),
+                )
+
+        def regroup(eng_copy, r, n0, n1):
+            ci, g = divmod(r, 2)
+            src = raw[ci][:, 4 * g : 4 * g + 4, n0:n1]
+            dst = grp[ci][:, g, n0:n1, :]
+            eng_copy(
+                out=dst.rearrange("p (c i) t -> p c t i", i=4),
+                in_=src.rearrange("p t (c i) -> p c t i", i=4),
+            )
+
+        def rg_v(r):
+            ci, g = divmod(r, 2)
+            if g == 0:
+                grp[ci] = grp_pool.tile([P, 2, 512, 4], BF16, name="grp", align_bytes=64)
+            regroup(nc.vector.tensor_copy, r, 0, V_COLS)
+
+        def rg_s(r):
+            regroup(nc.scalar.copy, r, V_COLS, 512)
+
+        def cq(r):
+            ci, g = divmod(r, 2)
+            if ci < 2:
+                codes, scales = w_codes[:, ci, g, :], w_scales[:, ci, g, :]
+            else:
+                codes, scales = hw_codes[:, ci - 2, g, :], hw_scales[:, ci - 2, g, :]
+            nc.vector.quantize_mx(
+                out=codes.bitcast(FP8X4),
+                scales=scales,
+                in_=grp[ci][:, g, :, :].rearrange("p n j -> p (n j)"),
+            )
+
+        def hdn_t(q):
+            n, g = divmod(q, 2)
+            xts[q] = []
+            for tp in range(2):
+                xt = ps_xt.tile([P, 2, 256], F32, name="xt")
+                for u in range(2):
+                    for t2 in range(2):
+                        a = 2 * g + u
+                        nc.tensor.transpose(
+                            out=xt[:, u, P * t2 : P * t2 + P],
+                            in_=hr[n][:, 2 * tp + t2, :].bitcast(F32)[:, P * a : P * a + P],
+                            identity=ident_f[:],
+                        )
+                xts[q].append(xt)
+
+        def t_out(q):
+            n, g = divmod(q, 2)
+            if g == 0:
+                hg[n] = hg_pool.tile([P, 2, 2048], BF16, name="hg", align_bytes=64)
+            g32 = hg[n][:, g, :].bitcast(F32)
+            for tp in range(2):
+                nc.scalar.copy(
+                    out=g32[:, 512 * tp : 512 * tp + 512].rearrange("p (c u) -> p c u", u=2),
+                    in_=xts[q][tp][:].rearrange("p u c -> p c u"),
+                )
+
+        def hq(q):
+            n, g = divmod(q, 2)
+            if g == 0:
+                hc[n] = hc_pool.tile([P, 2, 512], U32, name="hc", align_bytes=64)
+                hs[n] = hc_pool.tile([P, 2, 512], U8, name="hs", align_bytes=64)
+            nc.vector.quantize_mx(out=hc[n][:, g, :].bitcast(FP8X4), scales=hs[n][:, g, :], in_=hg[n][:, g, :])
+
+        def mx(k):
+            n, h = divmod(k, 2)
+            banks[k] = []
+            for mm in range(4):
+                ps = ps_mm.tile([P, 512], F32, name="mm")
+                for g in range(2):
+                    nc.tensor.matmul_mx(
+                        out=ps[:],
+                        lhsT=w_codes[:, h, g, P * mm : P * mm + P].bitcast(FP8X4),
+                        lhsT_scale=w_scales[:, h, g, P * mm : P * mm + P],
+                        rhs=hc[n][:, g, :].bitcast(FP8X4),
+                        rhs_scale=hs[n][:, g, :],
+                        start=(g == 0),
+                        stop=(g == 1),
+                    )
+                banks[k].append(ps)
+
+        def sq(k):
+            h = k % 2
+            s4[k] = s_pool.tile([P, 4, 512], F32, name="s4")
+            for mm in range(4):
+                m = 4 * h + mm
+                nc.scalar.activation(
+                    out=s4[k][:, mm, :], in_=banks[k][mm][:], func=ACT.Square, bias=bias[:, m : m + 1], scale=1.0
+                )
+
+        def cube(k):
+            h = k % 2
+            c4[k] = c_pool.tile([P, 4, 512], F32, name="c4")
+            for mm in range(4):
+                m = 4 * h + mm
+                nc.vector.scalar_tensor_tensor(
+                    out=c4[k][:, mm, :],
+                    in0=banks[k][mm][:],
+                    scalar=bias[:, m : m + 1],
+                    in1=s4[k][:, mm, :],
+                    op0=ALU.add,
+                    op1=ALU.mult,
+                )
+                nc.gpsimd.tensor_scalar(
+                    out=c4[k][:, mm, :], in0=c4[k][:, mm, :], scalar1=BIG, scalar2=EPS3, op0=ALU.min, op1=ALU.max
+                )
+
+        def sum_t(k):
+            n, h = divmod(k, 2)
+            for mm in range(4):
+                for ts in range(4):
+                    nc.tensor.matmul(
+                        out=sums[h][:, P * mm : P * mm + P],
+                        lhsT=c4[k][:, mm, P * ts : P * ts + P],
+                        rhs=ident_f[:],
+                        is_transpose=True,
+                        start=(n == 0 and mm == 0 and ts == 0),
+                        stop=(n == 8 and mm == 3 and ts == 3),
+                    )
+
+        make_identity(nc, ident_f[:])
+        make_identity(nc, ident_b[:])
+        nc.vector.memset(brow[:], 0.0)
+        nc.vector.memset(one[:], 1.0)
+        nc.scalar.dma_start(out=brow[0:8, :], in_=fc2_b.rearrange("(m p) -> m p", p=P))
+        load_h(0)
+        load_chunk(0)
+        load_h(1)
+        load_chunk(1)
+        load_h(2)
+        load_chunk(2)
+
+        bt = ps_xt.tile([P, P], BF16, name="xt")
+        nc.tensor.transpose(out=bt[:], in_=brow[:], identity=ident_b[:])
+        nc.vector.tensor_copy(out=bias[:], in_=bt[:, 0:8])
+
+        hdn_t(0)
+        t_out(0)
+        hdn_t(1)
+        t_out(1)
+        load_h(3)
+        hq(0)
+        hq(1)
+        rg_v(0)
+        rg_s(0)
+        rg_v(1)
+        rg_s(1)
+        cq(0)
+        cq(1)
+        hdn_t(2)
+
+        for k in range(NSTEP):
+            mx(k)
+            if k + 2 < NPART:
+                t_out(k + 2)
+            sq(k)
+            if k == 0:
+                rg_v(2)
+                rg_s(2)
+                rg_v(3)
+                rg_s(3)
+                load_chunk(3)
+                load_chunk(4)
+                hq(2)
+                cq(2)
+                cq(3)
+            else:
+                if 4 <= k + 2 <= 19:
+                    cq(k + 2)
+                if 4 <= k + 3 <= 19:
+                    rg_v(k + 3)
+                if k + 2 < NPART:
+                    hq(k + 2)
+            cube(k)
+            if k >= 1:
+                sum_t(k - 1)
+            if k + 3 < NPART:
+                hdn_t(k + 3)
+            if k >= 1 and 4 <= k + 3 <= 19:
+                rg_s(k + 3)
+            if k % 2 == 0:
+                if k // 2 + 4 <= 8:
+                    load_h(k // 2 + 4)
+                if k >= 2 and k // 2 + 4 <= 9:
+                    load_chunk(k // 2 + 4)
+            if k == 12:
+                nc.sync.dma_start(out=hb[:], in_=head_b.partition_broadcast(P))
+
+        nc.scalar.activation(out=lng[:, 0:512], in_=sums[0][:], func=ACT.Ln, scale=1.0 / NT)
+        sum_t(NSTEP - 1)
+        nc.scalar.activation(out=lng[:, 512:1024], in_=sums[1][:], func=ACT.Ln, scale=1.0 / NT)
+        for g in range(2):
+            nc.scalar.activation(
+                out=gb[:, 512 * g : 512 * g + 512], in_=lng[:, 512 * g : 512 * g + 512], func=ACT.Exp, scale=1.0 / 3.0
+            )
+            gt = ps_xt.tile([P, 4, P], BF16, name="xt")
+            for j in range(4):
+                a = 4 * g + j
+                nc.tensor.transpose(out=gt[:, j, :], in_=gb[:, P * a : P * a + P], identity=ident_b[:])
+            nc.vector.tensor_copy(out=g_grp[:, g, :, :], in_=gt[:].rearrange("p j b -> p b j"))
+        nc.scalar.activation(out=dmy[:], in_=one[:], func=ACT.Sqrt)
+        for g in range(2):
+            nc.vector.quantize_mx(
+                out=g_codes[:, g, :].bitcast(FP8X4),
+                scales=g_scales[:, g, :],
+                in_=g_grp[:, g, :, :].rearrange("p b j -> p (b j)"),
+            )
+        for nt in range(8):
+            ps = ps_mm.tile([P, 512], F32, name="mm")
+            for g in range(2):
+                nc.tensor.matmul_mx(
+                    out=ps[:],
+                    lhsT=g_codes[:, g, :].bitcast(FP8X4),
+                    lhsT_scale=g_scales[:, g, :],
+                    rhs=hw_codes[:, nt, g, :].bitcast(FP8X4),
+                    rhs_scale=hw_scales[:, nt, g, :],
+                    start=(g == 0),
+                    stop=(g == 1),
+                )
+            cols = slice(512 * nt, 512 * nt + 512)
+            nc.vector.tensor_tensor(out=d[:, cols], in0=ps[:], in1=hb[:, cols], op=ALU.add)
+            nc.scalar.activation(out=junk[:], in_=d[:, cols], func=ACT.Square, accum_out=ss[:, nt : nt + 1])
+        nc.vector.tensor_reduce(out=tot[:], in_=ss[:], axis=AX.X, op=ALU.add)
+        nc.scalar.activation(out=nrm[:], in_=tot[:], func=ACT.Sqrt)
+        nc.vector.tensor_scalar_max(out=nrm[:], in0=nrm[:], scalar1=1e-12)
+        nc.vector.reciprocal(out=rinv[:], in_=nrm[:])
+        for q in range(4):
+            cols = slice(1024 * q, 1024 * q + 1024)
+            if q % 2 == 0:
+                nc.vector.tensor_scalar_mul(out=d[:, cols], in0=d[:, cols], scalar1=rinv[:, 0:1])
+            else:
+                nc.scalar.activation(out=d[:, cols], in_=d[:, cols], func=ACT.Copy, scale=rinv[:, 0:1])
+            nc.sync.dma_start(out=out[:, cols], in_=d[:, cols])

@@ -22,7 +22,8 @@ EPS3 = 1e-18
 BIG = 3.0e38
 NSTEP = 18
 NPART = 18
-V_COLS = 320
+V_COLS = 240
+S_MID = 376
 
 FLOPS = 2 * NB * NT * NF * NCH + 2 * NB * NCH * NOUT
 
@@ -111,8 +112,11 @@ def tile_tokenmudule_pb_kernel(tc, hdn, fc2_w, fc2_b, head_w, head_b, out):
                 grp[ci] = grp_pool.tile([P, 2, 512, 4], BF16, name="grp", align_bytes=64)
             regroup(nc.vector.tensor_copy, r, 0, V_COLS)
 
-        def rg_s(r):
-            regroup(nc.scalar.copy, r, V_COLS, 512)
+        def rg_s(r, piece):
+            if piece == 0:
+                regroup(nc.scalar.copy, r, V_COLS, S_MID)
+            else:
+                regroup(nc.scalar.copy, r, S_MID, 512)
 
         def cq(r):
             ci, g = divmod(r, 2)
@@ -126,31 +130,28 @@ def tile_tokenmudule_pb_kernel(tc, hdn, fc2_w, fc2_b, head_w, head_b, out):
                 in_=grp[ci][:, g, :, :].rearrange("p n j -> p (n j)"),
             )
 
-        def hdn_t(q):
+        def hdn_t(q, tp):
             n, g = divmod(q, 2)
-            xts[q] = []
-            for tp in range(2):
-                xt = ps_xt.tile([P, 2, 256], F32, name="xt")
-                for u in range(2):
-                    for t2 in range(2):
-                        a = 2 * g + u
-                        nc.tensor.transpose(
-                            out=xt[:, u, P * t2 : P * t2 + P],
-                            in_=hr[n][:, 2 * tp + t2, :].bitcast(F32)[:, P * a : P * a + P],
-                            identity=ident_f[:],
-                        )
-                xts[q].append(xt)
+            xt = ps_xt.tile([P, 2, 256], F32, name="xt")
+            for u in range(2):
+                for t2 in range(2):
+                    a = 2 * g + u
+                    nc.tensor.transpose(
+                        out=xt[:, u, P * t2 : P * t2 + P],
+                        in_=hr[n][:, 2 * tp + t2, :].bitcast(F32)[:, P * a : P * a + P],
+                        identity=ident_f[:],
+                    )
+            xts[(q, tp)] = xt
 
-        def t_out(q):
+        def t_out(q, tp):
             n, g = divmod(q, 2)
-            if g == 0:
+            if g == 0 and tp == 0:
                 hg[n] = hg_pool.tile([P, 2, 2048], BF16, name="hg", align_bytes=64)
             g32 = hg[n][:, g, :].bitcast(F32)
-            for tp in range(2):
-                nc.scalar.copy(
-                    out=g32[:, 512 * tp : 512 * tp + 512].rearrange("p (c u) -> p c u", u=2),
-                    in_=xts[q][tp][:].rearrange("p u c -> p c u"),
-                )
+            nc.scalar.copy(
+                out=g32[:, 512 * tp : 512 * tp + 512].rearrange("p (c u) -> p c u", u=2),
+                in_=xts[(q, tp)][:].rearrange("p u c -> p c u"),
+            )
 
         def hq(q):
             n, g = divmod(q, 2)
@@ -159,10 +160,9 @@ def tile_tokenmudule_pb_kernel(tc, hdn, fc2_w, fc2_b, head_w, head_b, out):
                 hs[n] = hc_pool.tile([P, 2, 512], U8, name="hs", align_bytes=64)
             nc.vector.quantize_mx(out=hc[n][:, g, :].bitcast(FP8X4), scales=hs[n][:, g, :], in_=hg[n][:, g, :])
 
-        def mx(k):
+        def mx(k, mms):
             n, h = divmod(k, 2)
-            banks[k] = []
-            for mm in range(4):
+            for mm in mms:
                 ps = ps_mm.tile([P, 512], F32, name="mm")
                 for g in range(2):
                     nc.tensor.matmul_mx(
@@ -174,37 +174,41 @@ def tile_tokenmudule_pb_kernel(tc, hdn, fc2_w, fc2_b, head_w, head_b, out):
                         start=(g == 0),
                         stop=(g == 1),
                     )
-                banks[k].append(ps)
+                banks[(k, mm)] = ps
 
-        def sq(k):
-            h = k % 2
-            s4[k] = s_pool.tile([P, 4, 512], F32, name="s4")
-            for mm in range(4):
-                m = 4 * h + mm
-                nc.scalar.activation(
-                    out=s4[k][:, mm, :], in_=banks[k][mm][:], func=ACT.Square, bias=bias[:, m : m + 1], scale=1.0
-                )
+        def sq(k, mm):
+            m = 4 * (k % 2) + mm
+            if mm == 0:
+                s4[k] = s_pool.tile([P, 4, 512], F32, name="s4")
+            nc.scalar.activation(
+                out=s4[k][:, mm, :], in_=banks[(k, mm)][:], func=ACT.Square, bias=bias[:, m : m + 1], scale=1.0
+            )
 
-        def cube(k):
-            h = k % 2
-            c4[k] = c_pool.tile([P, 4, 512], F32, name="c4")
-            for mm in range(4):
-                m = 4 * h + mm
-                nc.vector.scalar_tensor_tensor(
-                    out=c4[k][:, mm, :],
-                    in0=banks[k][mm][:],
-                    scalar=bias[:, m : m + 1],
-                    in1=s4[k][:, mm, :],
-                    op0=ALU.add,
-                    op1=ALU.mult,
-                )
-                nc.gpsimd.tensor_scalar(
-                    out=c4[k][:, mm, :], in0=c4[k][:, mm, :], scalar1=BIG, scalar2=EPS3, op0=ALU.min, op1=ALU.max
-                )
+        def stt(k, mm):
+            m = 4 * (k % 2) + mm
+            if mm == 0:
+                c4[k] = c_pool.tile([P, 4, 512], F32, name="c4")
+            nc.vector.scalar_tensor_tensor(
+                out=c4[k][:, mm, :],
+                in0=banks[(k, mm)][:],
+                scalar=bias[:, m : m + 1],
+                in1=s4[k][:, mm, :],
+                op0=ALU.add,
+                op1=ALU.mult,
+            )
 
-        def sum_t(k):
+        def clamp_g(k, mm):
+            nc.gpsimd.tensor_scalar(
+                out=c4[k][:, mm, :], in0=c4[k][:, mm, :], scalar1=BIG, scalar2=EPS3, op0=ALU.min, op1=ALU.max
+            )
+
+        def clamp_v(k):
+            both = c4[k][:, 2:4, :].rearrange("p m c -> p (m c)")
+            nc.vector.tensor_scalar_max(out=both, in0=both, scalar1=EPS3)
+
+        def sum_t(k, mms):
             n, h = divmod(k, 2)
-            for mm in range(4):
+            for mm in mms:
                 for ts in range(4):
                     nc.tensor.matmul(
                         out=sums[h][:, P * mm : P * mm + P],
@@ -222,8 +226,8 @@ def tile_tokenmudule_pb_kernel(tc, hdn, fc2_w, fc2_b, head_w, head_b, out):
         nc.scalar.dma_start(out=brow[0:8, :], in_=fc2_b.rearrange("(m p) -> m p", p=P))
         load_h(0)
         load_chunk(0)
-        load_h(1)
         load_chunk(1)
+        load_h(1)
         load_h(2)
         load_chunk(2)
 
@@ -231,50 +235,75 @@ def tile_tokenmudule_pb_kernel(tc, hdn, fc2_w, fc2_b, head_w, head_b, out):
         nc.tensor.transpose(out=bt[:], in_=brow[:], identity=ident_b[:])
         nc.vector.tensor_copy(out=bias[:], in_=bt[:, 0:8])
 
-        hdn_t(0)
-        t_out(0)
-        hdn_t(1)
-        t_out(1)
+        for q in range(2):
+            for tp in range(2):
+                hdn_t(q, tp)
+            for tp in range(2):
+                t_out(q, tp)
         load_h(3)
         hq(0)
         hq(1)
-        rg_v(0)
-        rg_s(0)
-        rg_v(1)
-        rg_s(1)
+        for r in range(2):
+            rg_v(r)
+            rg_s(r, 0)
+            rg_s(r, 1)
         cq(0)
         cq(1)
-        hdn_t(2)
 
         for k in range(NSTEP):
-            mx(k)
-            if k + 2 < NPART:
-                t_out(k + 2)
-            sq(k)
+            chunk_work = k >= 1 and 4 <= k + 3 <= 19
+            mx(k, [0, 1])
+            if k >= 2:
+                sum_t(k - 2, [2, 3])
             if k == 0:
-                rg_v(2)
-                rg_s(2)
-                rg_v(3)
-                rg_s(3)
+                hdn_t(2, 0)
+                hdn_t(2, 1)
+                for r in range(2, 4):
+                    rg_v(r)
+                    rg_s(r, 0)
+                    rg_s(r, 1)
                 load_chunk(3)
                 load_chunk(4)
-                hq(2)
+            else:
+                if k + 3 < NPART:
+                    hdn_t(k + 3, 0)
+                if k + 2 < NPART:
+                    t_out(k + 2, 1)
+            sq(k, 0)
+            sq(k, 1)
+            if k == 0:
+                t_out(2, 0)
+                t_out(2, 1)
                 cq(2)
                 cq(3)
             else:
-                if 4 <= k + 2 <= 19:
-                    cq(k + 2)
-                if 4 <= k + 3 <= 19:
-                    rg_v(k + 3)
-                if k + 2 < NPART:
-                    hq(k + 2)
-            cube(k)
+                clamp_v(k - 1)
+            if k + 2 < NPART:
+                hq(k + 2)
+            if k >= 1 and 4 <= k + 2 <= 19:
+                cq(k + 2)
+            if chunk_work:
+                rg_v(k + 3)
+                rg_s(k + 3, 0)
+            mx(k, [2, 3])
             if k >= 1:
-                sum_t(k - 1)
+                sum_t(k - 1, [0, 1])
+            if k == 0:
+                hdn_t(3, 0)
+            elif k + 3 < NPART:
+                hdn_t(k + 3, 1)
             if k + 3 < NPART:
-                hdn_t(k + 3)
-            if k >= 1 and 4 <= k + 3 <= 19:
-                rg_s(k + 3)
+                t_out(k + 3, 0)
+            if k == 0:
+                hdn_t(3, 1)
+            sq(k, 2)
+            sq(k, 3)
+            if chunk_work:
+                rg_s(k + 3, 1)
+            for mm in range(4):
+                stt(k, mm)
+                if mm < 2:
+                    clamp_g(k, mm)
             if k % 2 == 0:
                 if k // 2 + 4 <= 8:
                     load_h(k // 2 + 4)
@@ -283,9 +312,28 @@ def tile_tokenmudule_pb_kernel(tc, hdn, fc2_w, fc2_b, head_w, head_b, out):
             if k == 12:
                 nc.sync.dma_start(out=hb[:], in_=head_b.partition_broadcast(P))
 
+        clamp_v(NSTEP - 1)
+        sum_t(NSTEP - 2, [2, 3])
         nc.scalar.activation(out=lng[:, 0:512], in_=sums[0][:], func=ACT.Ln, scale=1.0 / NT)
-        sum_t(NSTEP - 1)
+        sum_t(NSTEP - 1, [0, 1])
+        sum_t(NSTEP - 1, [2, 3])
         nc.scalar.activation(out=lng[:, 512:1024], in_=sums[1][:], func=ACT.Ln, scale=1.0 / NT)
+
+        ps2 = {}
+
+        def head_pass(nt, g):
+            if g == 0:
+                ps2[nt] = ps_mm.tile([P, 512], F32, name="mm")
+            nc.tensor.matmul_mx(
+                out=ps2[nt][:],
+                lhsT=g_codes[:, g, :].bitcast(FP8X4),
+                lhsT_scale=g_scales[:, g, :],
+                rhs=hw_codes[:, nt, g, :].bitcast(FP8X4),
+                rhs_scale=hw_scales[:, nt, g, :],
+                start=(g == 0),
+                stop=(g == 1),
+            )
+
         for g in range(2):
             nc.scalar.activation(
                 out=gb[:, 512 * g : 512 * g + 512], in_=lng[:, 512 * g : 512 * g + 512], func=ACT.Exp, scale=1.0 / 3.0
@@ -295,36 +343,30 @@ def tile_tokenmudule_pb_kernel(tc, hdn, fc2_w, fc2_b, head_w, head_b, out):
                 a = 4 * g + j
                 nc.tensor.transpose(out=gt[:, j, :], in_=gb[:, P * a : P * a + P], identity=ident_b[:])
             nc.vector.tensor_copy(out=g_grp[:, g, :, :], in_=gt[:].rearrange("p j b -> p b j"))
-        nc.scalar.activation(out=dmy[:], in_=one[:], func=ACT.Sqrt)
-        for g in range(2):
             nc.vector.quantize_mx(
                 out=g_codes[:, g, :].bitcast(FP8X4),
                 scales=g_scales[:, g, :],
                 in_=g_grp[:, g, :, :].rearrange("p b j -> p (b j)"),
             )
+            if g == 0:
+                for nt in range(4):
+                    head_pass(nt, 0)
+        nc.scalar.activation(out=dmy[:], in_=one[:], func=ACT.Sqrt)
         for nt in range(8):
-            ps = ps_mm.tile([P, 512], F32, name="mm")
-            for g in range(2):
-                nc.tensor.matmul_mx(
-                    out=ps[:],
-                    lhsT=g_codes[:, g, :].bitcast(FP8X4),
-                    lhsT_scale=g_scales[:, g, :],
-                    rhs=hw_codes[:, nt, g, :].bitcast(FP8X4),
-                    rhs_scale=hw_scales[:, nt, g, :],
-                    start=(g == 0),
-                    stop=(g == 1),
-                )
+            if nt >= 4:
+                head_pass(nt, 0)
+            head_pass(nt, 1)
             cols = slice(512 * nt, 512 * nt + 512)
-            nc.vector.tensor_tensor(out=d[:, cols], in0=ps[:], in1=hb[:, cols], op=ALU.add)
+            nc.vector.tensor_tensor(out=d[:, cols], in0=ps2[nt][:], in1=hb[:, cols], op=ALU.add)
             nc.scalar.activation(out=junk[:], in_=d[:, cols], func=ACT.Square, accum_out=ss[:, nt : nt + 1])
         nc.vector.tensor_reduce(out=tot[:], in_=ss[:], axis=AX.X, op=ALU.add)
         nc.scalar.activation(out=nrm[:], in_=tot[:], func=ACT.Sqrt)
         nc.vector.tensor_scalar_max(out=nrm[:], in0=nrm[:], scalar1=1e-12)
         nc.vector.reciprocal(out=rinv[:], in_=nrm[:])
-        for q in range(4):
-            cols = slice(1024 * q, 1024 * q + 1024)
-            if q % 2 == 0:
-                nc.vector.tensor_scalar_mul(out=d[:, cols], in0=d[:, cols], scalar1=rinv[:, 0:1])
-            else:
+        for nt in range(8):
+            cols = slice(512 * nt, 512 * nt + 512)
+            if nt % 3 == 1:
                 nc.scalar.activation(out=d[:, cols], in_=d[:, cols], func=ACT.Copy, scale=rinv[:, 0:1])
+            else:
+                nc.vector.tensor_scalar_mul(out=d[:, cols], in0=d[:, cols], scalar1=rinv[:, 0:1])
             nc.sync.dma_start(out=out[:, cols], in_=d[:, cols])

@@ -22,8 +22,8 @@ EPS3 = 1e-18
 BIG = 3.0e38
 NSTEP = 18
 NPART = 18
-V_COLS = 240
-S_MID = 376
+BUSY_SPLIT = (120, 160)
+IDLE_SPLIT = (240, 160)
 
 FLOPS = 2 * NB * NT * NF * NCH + 2 * NB * NCH * NOUT
 
@@ -86,10 +86,11 @@ def tile_tokenmudule_pb_kernel(tc, hdn, fc2_w, fc2_b, head_w, head_b, out):
         def load_chunk(ci):
             raw[ci] = raw_pool.tile([P, 8, 512], BF16, name="raw")
             if ci < 2:
-                src = fc2_w[:, 512 * ci : 512 * ci + 512].rearrange("(a p e) c -> e p a c", a=4, p=P, e=2)
-                dst = raw[ci][:].rearrange("p (a e) c -> p a e c", e=2)
-                for e in range(2):
-                    nc.sync.dma_start(out=dst[:, :, e, :], in_=src[e])
+                for a in range(4):
+                    nc.sync.dma_start(
+                        out=raw[ci][:, 2 * a : 2 * a + 2, :],
+                        in_=fc2_w[256 * a : 256 * a + 256, 512 * ci : 512 * ci + 512].rearrange("(p e) c -> p e c", e=2),
+                    )
             else:
                 nt = ci - 2
                 nc.sync.dma_start(
@@ -97,26 +98,28 @@ def tile_tokenmudule_pb_kernel(tc, hdn, fc2_w, fc2_b, head_w, head_b, out):
                     in_=head_w[:, 512 * nt : 512 * nt + 512].rearrange("(a p) n -> p a n", a=8, p=P),
                 )
 
-        def regroup(eng_copy, r, n0, n1):
+        def regroup_views(r, n0, n1):
             ci, g = divmod(r, 2)
             src = raw[ci][:, 4 * g : 4 * g + 4, n0:n1]
             dst = grp[ci][:, g, n0:n1, :]
-            eng_copy(
-                out=dst.rearrange("p (c i) t -> p c t i", i=4),
-                in_=src.rearrange("p t (c i) -> p c t i", i=4),
-            )
+            return dst.rearrange("p (c i) t -> p c t i", i=4), src.rearrange("p t (c i) -> p c t i", i=4)
 
-        def rg_v(r):
+        def rg_v(r, split):
             ci, g = divmod(r, 2)
             if g == 0:
                 grp[ci] = grp_pool.tile([P, 2, 512, 4], BF16, name="grp", align_bytes=64)
-            regroup(nc.vector.tensor_copy, r, 0, V_COLS)
+            dst, src = regroup_views(r, 0, split[0])
+            nc.vector.tensor_copy(out=dst, in_=src)
 
-        def rg_s(r, piece):
-            if piece == 0:
-                regroup(nc.scalar.copy, r, V_COLS, S_MID)
-            else:
-                regroup(nc.scalar.copy, r, S_MID, 512)
+        def rg_g(r, split):
+            dst, src = regroup_views(r, split[0], split[0] + split[1])
+            nc.gpsimd.tensor_scalar(out=dst, in0=src, scalar1=1.0, scalar2=0.0, op0=ALU.mult, op1=ALU.add)
+
+        def rg_s(r, split, piece, pieces):
+            n0 = split[0] + split[1]
+            width = (512 - n0) // pieces
+            dst, src = regroup_views(r, n0 + piece * width, n0 + (piece + 1) * width)
+            nc.scalar.copy(out=dst, in_=src)
 
         def cq(r):
             ci, g = divmod(r, 2)
@@ -235,6 +238,11 @@ def tile_tokenmudule_pb_kernel(tc, hdn, fc2_w, fc2_b, head_w, head_b, out):
         nc.tensor.transpose(out=bt[:], in_=brow[:], identity=ident_b[:])
         nc.vector.tensor_copy(out=bias[:], in_=bt[:, 0:8])
 
+        def regroup_idle(r):
+            rg_v(r, IDLE_SPLIT)
+            rg_g(r, IDLE_SPLIT)
+            rg_s(r, IDLE_SPLIT, 0, 1)
+
         for q in range(2):
             for tp in range(2):
                 hdn_t(q, tp)
@@ -243,25 +251,27 @@ def tile_tokenmudule_pb_kernel(tc, hdn, fc2_w, fc2_b, head_w, head_b, out):
         load_h(3)
         hq(0)
         hq(1)
-        for r in range(2):
-            rg_v(r)
-            rg_s(r, 0)
-            rg_s(r, 1)
+        regroup_idle(0)
+        regroup_idle(1)
         cq(0)
         cq(1)
 
+        rg_at = {}
+        for k in range(1, 16):
+            if k != 8:
+                rg_at[k] = 4 + len(rg_at)
+
         for k in range(NSTEP):
-            chunk_work = k >= 1 and 4 <= k + 3 <= 19
+            r_new = rg_at.get(k)
+            r_old = rg_at.get(k - 1)
             mx(k, [0, 1])
             if k >= 2:
                 sum_t(k - 2, [2, 3])
             if k == 0:
                 hdn_t(2, 0)
                 hdn_t(2, 1)
-                for r in range(2, 4):
-                    rg_v(r)
-                    rg_s(r, 0)
-                    rg_s(r, 1)
+                regroup_idle(2)
+                regroup_idle(3)
                 load_chunk(3)
                 load_chunk(4)
             else:
@@ -278,13 +288,16 @@ def tile_tokenmudule_pb_kernel(tc, hdn, fc2_w, fc2_b, head_w, head_b, out):
                 cq(3)
             else:
                 clamp_v(k - 1)
-            if k + 2 < NPART:
-                hq(k + 2)
-            if k >= 1 and 4 <= k + 2 <= 19:
-                cq(k + 2)
-            if chunk_work:
-                rg_v(k + 3)
-                rg_s(k + 3, 0)
+                if k == 1:
+                    hq(2)
+                if k + 2 < NPART:
+                    hq(k + 2)
+            if r_old is not None:
+                cq(r_old)
+            if r_new is not None:
+                rg_v(r_new, BUSY_SPLIT)
+                rg_g(r_new, BUSY_SPLIT)
+                rg_s(r_new, BUSY_SPLIT, 0, 2)
             mx(k, [2, 3])
             if k >= 1:
                 sum_t(k - 1, [0, 1])
@@ -298,26 +311,29 @@ def tile_tokenmudule_pb_kernel(tc, hdn, fc2_w, fc2_b, head_w, head_b, out):
                 hdn_t(3, 1)
             sq(k, 2)
             sq(k, 3)
-            if chunk_work:
-                rg_s(k + 3, 1)
+            if r_new is not None:
+                rg_s(r_new, BUSY_SPLIT, 1, 2)
+                if r_new % 2 == 1 and r_new // 2 + 3 <= 9:
+                    load_chunk(r_new // 2 + 3)
             for mm in range(4):
                 stt(k, mm)
                 if mm < 2:
                     clamp_g(k, mm)
-            if k % 2 == 0:
-                if k // 2 + 4 <= 8:
-                    load_h(k // 2 + 4)
-                if k >= 2 and k // 2 + 4 <= 9:
-                    load_chunk(k // 2 + 4)
+            if k % 2 == 0 and k // 2 + 4 <= 8:
+                load_h(k // 2 + 4)
             if k == 12:
                 nc.sync.dma_start(out=hb[:], in_=head_b.partition_broadcast(P))
 
         clamp_v(NSTEP - 1)
+        regroup_idle(18)
+        regroup_idle(19)
         sum_t(NSTEP - 2, [2, 3])
         nc.scalar.activation(out=lng[:, 0:512], in_=sums[0][:], func=ACT.Ln, scale=1.0 / NT)
         sum_t(NSTEP - 1, [0, 1])
         sum_t(NSTEP - 1, [2, 3])
         nc.scalar.activation(out=lng[:, 512:1024], in_=sums[1][:], func=ACT.Ln, scale=1.0 / NT)
+        cq(18)
+        cq(19)
 
         ps2 = {}
 

@@ -63,6 +63,7 @@ def tile_tokenmudule_pb_kernel(tc, hdn, fc2_w, fc2_b, head_w, head_b, out):
         g_codes = const.tile([P, 2, P], U32, align_bytes=64)
         g_scales = const.tile([P, 2, P], U8, align_bytes=64)
         ss = const.tile([P, 8], F32)
+        accv = const.tile([P, 2, 1024], F32)
         tot = const.tile([P, 1], F32)
         nrm = const.tile([P, 1], F32)
         rinv = const.tile([P, 1], F32)
@@ -206,8 +207,27 @@ def tile_tokenmudule_pb_kernel(tc, hdn, fc2_w, fc2_b, head_w, head_b, out):
             )
 
         def clamp_v(k):
+            n, h = divmod(k, 2)
             both = c4[k][:, 2:4, :].rearrange("p m c -> p (m c)")
-            nc.vector.tensor_scalar_max(out=both, in0=both, scalar1=EPS3)
+            if n == 0:
+                nc.vector.tensor_scalar_max(out=accv[:, h, :], in0=both, scalar1=EPS3)
+            else:
+                nc.vector.scalar_tensor_tensor(
+                    out=accv[:, h, :], in0=both, scalar=EPS3, in1=accv[:, h, :], op0=ALU.max, op1=ALU.add
+                )
+
+        def sum_acc(h):
+            for mm in range(2, 4):
+                for ts in range(4):
+                    c0 = 512 * (mm - 2) + P * ts
+                    nc.tensor.matmul(
+                        out=sums[h][:, P * mm : P * mm + P],
+                        lhsT=accv[:, h, c0 : c0 + P],
+                        rhs=ident_f[:],
+                        is_transpose=True,
+                        start=False,
+                        stop=(mm == 3 and ts == 3),
+                    )
 
         def sum_t(k, mms):
             n, h = divmod(k, 2)
@@ -219,7 +239,7 @@ def tile_tokenmudule_pb_kernel(tc, hdn, fc2_w, fc2_b, head_w, head_b, out):
                         rhs=ident_f[:],
                         is_transpose=True,
                         start=(n == 0 and mm == 0 and ts == 0),
-                        stop=(n == 8 and mm == 3 and ts == 3),
+                        stop=False,
                     )
 
         make_identity(nc, ident_f[:])
@@ -266,7 +286,7 @@ def tile_tokenmudule_pb_kernel(tc, hdn, fc2_w, fc2_b, head_w, head_b, out):
             r_old = rg_at.get(k - 1)
             mx(k, [0, 1])
             if k >= 2:
-                sum_t(k - 2, [2, 3])
+                sum_t(k - 2, [1])
             if k == 0:
                 hdn_t(2, 0)
                 hdn_t(2, 1)
@@ -300,7 +320,7 @@ def tile_tokenmudule_pb_kernel(tc, hdn, fc2_w, fc2_b, head_w, head_b, out):
                 rg_s(r_new, BUSY_SPLIT, 0, 2)
             mx(k, [2, 3])
             if k >= 1:
-                sum_t(k - 1, [0, 1])
+                sum_t(k - 1, [0])
             if k == 0:
                 hdn_t(3, 0)
             elif k + 3 < NPART:
@@ -327,10 +347,11 @@ def tile_tokenmudule_pb_kernel(tc, hdn, fc2_w, fc2_b, head_w, head_b, out):
         clamp_v(NSTEP - 1)
         regroup_idle(18)
         regroup_idle(19)
-        sum_t(NSTEP - 2, [2, 3])
+        sum_t(NSTEP - 2, [1])
+        sum_acc(0)
         nc.scalar.activation(out=lng[:, 0:512], in_=sums[0][:], func=ACT.Ln, scale=1.0 / NT)
         sum_t(NSTEP - 1, [0, 1])
-        sum_t(NSTEP - 1, [2, 3])
+        sum_acc(1)
         nc.scalar.activation(out=lng[:, 512:1024], in_=sums[1][:], func=ACT.Ln, scale=1.0 / NT)
         cq(18)
         cq(19)

@@ -22,8 +22,8 @@ EPS3 = 1e-18
 BIG = 3.0e38
 NSTEP = 18
 NPART = 18
-BUSY_SPLIT = (120, 160)
-IDLE_SPLIT = (240, 160)
+V_COLS = 240
+S_MID = 376
 
 FLOPS = 2 * NB * NT * NF * NCH + 2 * NB * NCH * NOUT
 
@@ -58,12 +58,10 @@ def tile_tokenmudule_pb_kernel(tc, hdn, fc2_w, fc2_b, head_w, head_b, out):
         d = const.tile([P, NOUT], F32)
         junk = const.tile([P, 512], F32)
         lng = const.tile([P, NCH], F32)
-        gb = const.tile([P, NCH], BF16)
         g_grp = const.tile([P, 2, P, 4], BF16, align_bytes=64)
         g_codes = const.tile([P, 2, P], U32, align_bytes=64)
         g_scales = const.tile([P, 2, P], U8, align_bytes=64)
         ss = const.tile([P, 8], F32)
-        accv = const.tile([P, 2, 1024], F32)
         tot = const.tile([P, 1], F32)
         nrm = const.tile([P, 1], F32)
         rinv = const.tile([P, 1], F32)
@@ -87,11 +85,10 @@ def tile_tokenmudule_pb_kernel(tc, hdn, fc2_w, fc2_b, head_w, head_b, out):
         def load_chunk(ci):
             raw[ci] = raw_pool.tile([P, 8, 512], BF16, name="raw")
             if ci < 2:
-                for a in range(4):
-                    nc.sync.dma_start(
-                        out=raw[ci][:, 2 * a : 2 * a + 2, :],
-                        in_=fc2_w[256 * a : 256 * a + 256, 512 * ci : 512 * ci + 512].rearrange("(p e) c -> p e c", e=2),
-                    )
+                src = fc2_w[:, 512 * ci : 512 * ci + 512].rearrange("(a p e) c -> e p a c", a=4, p=P, e=2)
+                dst = raw[ci][:].rearrange("p (a e) c -> p a e c", e=2)
+                for e in range(2):
+                    nc.sync.dma_start(out=dst[:, :, e, :], in_=src[e])
             else:
                 nt = ci - 2
                 nc.sync.dma_start(
@@ -99,28 +96,26 @@ def tile_tokenmudule_pb_kernel(tc, hdn, fc2_w, fc2_b, head_w, head_b, out):
                     in_=head_w[:, 512 * nt : 512 * nt + 512].rearrange("(a p) n -> p a n", a=8, p=P),
                 )
 
-        def regroup_views(r, n0, n1):
+        def regroup(eng_copy, r, n0, n1):
             ci, g = divmod(r, 2)
             src = raw[ci][:, 4 * g : 4 * g + 4, n0:n1]
             dst = grp[ci][:, g, n0:n1, :]
-            return dst.rearrange("p (c i) t -> p c t i", i=4), src.rearrange("p t (c i) -> p c t i", i=4)
+            eng_copy(
+                out=dst.rearrange("p (c i) t -> p c t i", i=4),
+                in_=src.rearrange("p t (c i) -> p c t i", i=4),
+            )
 
-        def rg_v(r, split):
+        def rg_v(r):
             ci, g = divmod(r, 2)
             if g == 0:
                 grp[ci] = grp_pool.tile([P, 2, 512, 4], BF16, name="grp", align_bytes=64)
-            dst, src = regroup_views(r, 0, split[0])
-            nc.vector.tensor_copy(out=dst, in_=src)
+            regroup(nc.vector.tensor_copy, r, 0, V_COLS)
 
-        def rg_g(r, split):
-            dst, src = regroup_views(r, split[0], split[0] + split[1])
-            nc.gpsimd.tensor_scalar(out=dst, in0=src, scalar1=1.0, scalar2=0.0, op0=ALU.mult, op1=ALU.add)
-
-        def rg_s(r, split, piece, pieces):
-            n0 = split[0] + split[1]
-            width = (512 - n0) // pieces
-            dst, src = regroup_views(r, n0 + piece * width, n0 + (piece + 1) * width)
-            nc.scalar.copy(out=dst, in_=src)
+        def rg_s(r, piece):
+            if piece == 0:
+                regroup(nc.scalar.copy, r, V_COLS, S_MID)
+            else:
+                regroup(nc.scalar.copy, r, S_MID, 512)
 
         def cq(r):
             ci, g = divmod(r, 2)
@@ -207,27 +202,8 @@ def tile_tokenmudule_pb_kernel(tc, hdn, fc2_w, fc2_b, head_w, head_b, out):
             )
 
         def clamp_v(k):
-            n, h = divmod(k, 2)
             both = c4[k][:, 2:4, :].rearrange("p m c -> p (m c)")
-            if n == 0:
-                nc.vector.tensor_scalar_max(out=accv[:, h, :], in0=both, scalar1=EPS3)
-            else:
-                nc.vector.scalar_tensor_tensor(
-                    out=accv[:, h, :], in0=both, scalar=EPS3, in1=accv[:, h, :], op0=ALU.max, op1=ALU.add
-                )
-
-        def sum_acc(h):
-            for mm in range(2, 4):
-                for ts in range(4):
-                    c0 = 512 * (mm - 2) + P * ts
-                    nc.tensor.matmul(
-                        out=sums[h][:, P * mm : P * mm + P],
-                        lhsT=accv[:, h, c0 : c0 + P],
-                        rhs=ident_f[:],
-                        is_transpose=True,
-                        start=False,
-                        stop=(mm == 3 and ts == 3),
-                    )
+            nc.vector.tensor_scalar_max(out=both, in0=both, scalar1=EPS3)
 
         def sum_t(k, mms):
             n, h = divmod(k, 2)
@@ -239,7 +215,7 @@ def tile_tokenmudule_pb_kernel(tc, hdn, fc2_w, fc2_b, head_w, head_b, out):
                         rhs=ident_f[:],
                         is_transpose=True,
                         start=(n == 0 and mm == 0 and ts == 0),
-                        stop=False,
+                        stop=(n == 8 and mm == 3 and ts == 3),
                     )
 
         make_identity(nc, ident_f[:])
@@ -258,11 +234,6 @@ def tile_tokenmudule_pb_kernel(tc, hdn, fc2_w, fc2_b, head_w, head_b, out):
         nc.tensor.transpose(out=bt[:], in_=brow[:], identity=ident_b[:])
         nc.vector.tensor_copy(out=bias[:], in_=bt[:, 0:8])
 
-        def regroup_idle(r):
-            rg_v(r, IDLE_SPLIT)
-            rg_g(r, IDLE_SPLIT)
-            rg_s(r, IDLE_SPLIT, 0, 1)
-
         for q in range(2):
             for tp in range(2):
                 hdn_t(q, tp)
@@ -271,27 +242,25 @@ def tile_tokenmudule_pb_kernel(tc, hdn, fc2_w, fc2_b, head_w, head_b, out):
         load_h(3)
         hq(0)
         hq(1)
-        regroup_idle(0)
-        regroup_idle(1)
+        for r in range(2):
+            rg_v(r)
+            rg_s(r, 0)
+            rg_s(r, 1)
         cq(0)
         cq(1)
 
-        rg_at = {}
-        for k in range(1, 16):
-            if k != 8:
-                rg_at[k] = 4 + len(rg_at)
-
         for k in range(NSTEP):
-            r_new = rg_at.get(k)
-            r_old = rg_at.get(k - 1)
+            chunk_work = k >= 1 and 4 <= k + 3 <= 19
             mx(k, [0, 1])
             if k >= 2:
-                sum_t(k - 2, [1])
+                sum_t(k - 2, [2, 3])
             if k == 0:
                 hdn_t(2, 0)
                 hdn_t(2, 1)
-                regroup_idle(2)
-                regroup_idle(3)
+                for r in range(2, 4):
+                    rg_v(r)
+                    rg_s(r, 0)
+                    rg_s(r, 1)
                 load_chunk(3)
                 load_chunk(4)
             else:
@@ -308,19 +277,16 @@ def tile_tokenmudule_pb_kernel(tc, hdn, fc2_w, fc2_b, head_w, head_b, out):
                 cq(3)
             else:
                 clamp_v(k - 1)
-                if k == 1:
-                    hq(2)
-                if k + 2 < NPART:
-                    hq(k + 2)
-            if r_old is not None:
-                cq(r_old)
-            if r_new is not None:
-                rg_v(r_new, BUSY_SPLIT)
-                rg_g(r_new, BUSY_SPLIT)
-                rg_s(r_new, BUSY_SPLIT, 0, 2)
+            if k + 2 < NPART:
+                hq(k + 2)
+            if k >= 1 and 4 <= k + 2 <= 19:
+                cq(k + 2)
+            if chunk_work:
+                rg_v(k + 3)
+                rg_s(k + 3, 0)
             mx(k, [2, 3])
             if k >= 1:
-                sum_t(k - 1, [0])
+                sum_t(k - 1, [0, 1])
             if k == 0:
                 hdn_t(3, 0)
             elif k + 3 < NPART:
@@ -331,36 +297,30 @@ def tile_tokenmudule_pb_kernel(tc, hdn, fc2_w, fc2_b, head_w, head_b, out):
                 hdn_t(3, 1)
             sq(k, 2)
             sq(k, 3)
-            if r_new is not None:
-                rg_s(r_new, BUSY_SPLIT, 1, 2)
-                if r_new % 2 == 1 and r_new // 2 + 3 <= 9:
-                    load_chunk(r_new // 2 + 3)
+            if chunk_work:
+                rg_s(k + 3, 1)
             for mm in range(4):
                 stt(k, mm)
                 if mm < 2:
                     clamp_g(k, mm)
-            if k % 2 == 0 and k // 2 + 4 <= 8:
-                load_h(k // 2 + 4)
+            if k % 2 == 0:
+                if k // 2 + 4 <= 8:
+                    load_h(k // 2 + 4)
+                if k >= 2 and k // 2 + 4 <= 9:
+                    load_chunk(k // 2 + 4)
             if k == 12:
                 nc.sync.dma_start(out=hb[:], in_=head_b.partition_broadcast(P))
 
         clamp_v(NSTEP - 1)
-        regroup_idle(18)
-        regroup_idle(19)
-        sum_t(NSTEP - 2, [1])
-        sum_acc(0)
+        sum_t(NSTEP - 2, [2, 3])
         nc.scalar.activation(out=lng[:, 0:512], in_=sums[0][:], func=ACT.Ln, scale=1.0 / NT)
         sum_t(NSTEP - 1, [0, 1])
-        sum_acc(1)
+        sum_t(NSTEP - 1, [2, 3])
         nc.scalar.activation(out=lng[:, 512:1024], in_=sums[1][:], func=ACT.Ln, scale=1.0 / NT)
-        cq(18)
-        cq(19)
 
         ps2 = {}
 
         def head_pass(nt, g):
-            if g == 0:
-                ps2[nt] = ps_mm.tile([P, 512], F32, name="mm")
             nc.tensor.matmul_mx(
                 out=ps2[nt][:],
                 lhsT=g_codes[:, g, :].bitcast(FP8X4),
@@ -371,35 +331,42 @@ def tile_tokenmudule_pb_kernel(tc, hdn, fc2_w, fc2_b, head_w, head_b, out):
                 stop=(g == 1),
             )
 
+        lts = []
         for g in range(2):
-            nc.scalar.activation(
-                out=gb[:, 512 * g : 512 * g + 512], in_=lng[:, 512 * g : 512 * g + 512], func=ACT.Exp, scale=1.0 / 3.0
-            )
-            gt = ps_xt.tile([P, 4, P], BF16, name="xt")
+            lt = ps_xt.tile([P, 4, P], F32, name="xt")
             for j in range(4):
                 a = 4 * g + j
-                nc.tensor.transpose(out=gt[:, j, :], in_=gb[:, P * a : P * a + P], identity=ident_b[:])
-            nc.vector.tensor_copy(out=g_grp[:, g, :, :], in_=gt[:].rearrange("p j b -> p b j"))
+                nc.tensor.transpose(out=lt[:, j, :], in_=lng[:, P * a : P * a + P], identity=ident_f[:])
+            lts.append(lt)
+        for g in range(2):
+            nc.scalar.activation(
+                out=g_grp[:, g, :, :], in_=lts[g][:].rearrange("p j b -> p b j"), func=ACT.Exp, scale=1.0 / 3.0
+            )
             nc.vector.quantize_mx(
                 out=g_codes[:, g, :].bitcast(FP8X4),
                 scales=g_scales[:, g, :],
                 in_=g_grp[:, g, :, :].rearrange("p b j -> p (b j)"),
             )
             if g == 0:
-                for nt in range(4):
+                for nt in range(6):
+                    if nt < 4:
+                        ps2[nt] = ps_mm.tile([P, 512], F32, name="mm")
+                    else:
+                        ps2[nt] = ps_sum.tile([P, 512], F32, name="sum%d" % (nt - 4))
                     head_pass(nt, 0)
-        nc.scalar.activation(out=dmy[:], in_=one[:], func=ACT.Sqrt)
+        nc.scalar.activation(out=dmy[:], in_=one[:], func=ACT.Abs_reciprocal_sqrt)
         for nt in range(8):
-            if nt >= 4:
+            if nt >= 6:
+                ps2[nt] = ps_xt.tile([P, 512], F32, name="xt")
                 head_pass(nt, 0)
             head_pass(nt, 1)
+        for nt in range(8):
             cols = slice(512 * nt, 512 * nt + 512)
             nc.vector.tensor_tensor(out=d[:, cols], in0=ps2[nt][:], in1=hb[:, cols], op=ALU.add)
             nc.scalar.activation(out=junk[:], in_=d[:, cols], func=ACT.Square, accum_out=ss[:, nt : nt + 1])
-        nc.vector.tensor_reduce(out=tot[:], in_=ss[:], axis=AX.X, op=ALU.add)
-        nc.scalar.activation(out=nrm[:], in_=tot[:], func=ACT.Sqrt)
-        nc.vector.tensor_scalar_max(out=nrm[:], in0=nrm[:], scalar1=1e-12)
-        nc.vector.reciprocal(out=rinv[:], in_=nrm[:])
+        nc.scalar.activation(out=junk[:, 0:8], in_=ss[:], func=ACT.Identity, accum_out=tot[:])
+        nc.scalar.activation(out=nrm[:], in_=tot[:], func=ACT.Abs_reciprocal_sqrt)
+        nc.vector.tensor_scalar_min(out=rinv[:], in0=nrm[:], scalar1=1e12)
         for nt in range(8):
             cols = slice(512 * nt, 512 * nt + 512)
             if nt % 3 == 1:

from contextlib import ExitStack

import concourse.mybir as mybir
from concourse.masks import make_identity

F32 = mybir.dt.float32
BF16 = mybir.dt.bfloat16
U32 = mybir.dt.uint32
U8 = mybir.dt.uint8
FP8X4 = mybir.dt.float8_e4m3fn_x4
ALU = mybir.AluOpType
ACT = mybir.ActivationFunctionType
AX = mybir.AxisListType

P = 128
NB = 128
NT = 36
NF = 1024
NCH = 1024
NOUT = 4096
EPS3 = 1e-18
BIG = 3.0e38
NSTEP = 18
NPART = 18
V_COLS = 240
S_MID = 376

FLOPS = 2 * NB * NT * NF * NCH + 2 * NB * NCH * NOUT


def tile_tokenmudule_pb_kernel(tc, hdn, fc2_w, fc2_b, head_w, head_b, out):
    nc = tc.nc
    with ExitStack() as ctx:
        const = ctx.enter_context(tc.tile_pool(name="const", bufs=1))
        hr_pool = ctx.enter_context(tc.tile_pool(name="hr", bufs=3))
        hg_pool = ctx.enter_context(tc.tile_pool(name="hg", bufs=2))
        hc_pool = ctx.enter_context(tc.tile_pool(name="hc", bufs=3))
        raw_pool = ctx.enter_context(tc.tile_pool(name="raw", bufs=3))
        grp_pool = ctx.enter_context(tc.tile_pool(name="grp", bufs=2))
        s_pool = ctx.enter_context(tc.tile_pool(name="sq", bufs=2))
        c_pool = ctx.enter_context(tc.tile_pool(name="cube", bufs=3))
        ps_sum = ctx.enter_context(tc.psum_pool(name="pssum", bufs=1))
        ps_mm = ctx.enter_context(tc.psum_pool(name="psmm", bufs=4))
        ps_xt = ctx.enter_context(tc.psum_pool(name="psxt", bufs=2))
        ctx.enter_context(tc.manual_schedule())

        ident_f = const.tile([P, P], F32)
        ident_b = const.tile([P, P], BF16)
        brow = const.tile([P, P], BF16)
        bias = const.tile([P, 8], F32)
        one = const.tile([P, 1], F32)
        dmy = const.tile([P, 1], F32)
        w_codes = const.tile([P, 2, 2, 512], U32, align_bytes=64)
        w_scales = const.tile([P, 2, 2, 512], U8, align_bytes=64)
        hw_codes = const.tile([P, 8, 2, 512], U32, align_bytes=64)
        hw_scales = const.tile([P, 8, 2, 512], U8, align_bytes=64)
        hb = const.tile([P, NOUT], BF16)
        d = const.tile([P, NOUT], F32)
        junk = const.tile([P, 512], F32)
        lng = const.tile([P, NCH], F32)
        g_grp = const.tile([P, 2, P, 4], BF16, align_bytes=64)
        g_codes = const.tile([P, 2, P], U32, align_bytes=64)
        g_scales = const.tile([P, 2, P], U8, align_bytes=64)
        ss = const.tile([P, 8], F32)
        tot = const.tile([P, 1], F32)
        nrm = const.tile([P, 1], F32)
        rinv = const.tile([P, 1], F32)
        sums = [ps_sum.tile([P, 512], F32, name="sum%d" % i) for i in range(2)]

        hr = {}
        hg = {}
        hc = {}
        hs = {}
        raw = {}
        grp = {}
        xts = {}
        banks = {}
        s4 = {}
        c4 = {}

        def load_h(n):
            hr[n] = hr_pool.tile([P, 4, NF], BF16, name="hr")
            nc.sync.dma_start(out=hr[n][:], in_=hdn[:, 4 * n : 4 * n + 4, :])

        def load_chunk(ci):
            raw[ci] = raw_pool.tile([P, 8, 512], BF16, name="raw")
            if ci < 2:
                src = fc2_w[:, 512 * ci : 512 * ci + 512].rearrange("(a p e) c -> e p a c", a=4, p=P, e=2)
                dst = raw[ci][:].rearrange("p (a e) c -> p a e c", e=2)
                for e in range(2):
                    nc.sync.dma_start(out=dst[:, :, e, :], in_=src[e])
            else:
                nt = ci - 2
                nc.sync.dma_start(
                    out=raw[ci][:],
                    in_=head_w[:, 512 * nt : 512 * nt + 512].rearrange("(a p) n -> p a n", a=8, p=P),
                )

        def regroup(eng_copy, r, n0, n1):
            ci, g = divmod(r, 2)
            src = raw[ci][:, 4 * g : 4 * g + 4, n0:n1]
            dst = grp[ci][:, g, n0:n1, :]
            eng_copy(
                out=dst.rearrange("p (c i) t -> p c t i", i=4),
                in_=src.rearrange("p t (c i) -> p c t i", i=4),
            )

        def rg_v(r):
            ci, g = divmod(r, 2)
            if g == 0:
                grp[ci] = grp_pool.tile([P, 2, 512, 4], BF16, name="grp", align_bytes=64)
            regroup(nc.vector.tensor_copy, r, 0, V_COLS)

        def rg_s(r, piece):
            if piece == 0:
                regroup(nc.scalar.copy, r, V_COLS, S_MID)
            else:
                regroup(nc.scalar.copy, r, S_MID, 512)

        def cq(r):
            ci, g = divmod(r, 2)
            if ci < 2:
                codes, scales = w_codes[:, ci, g, :], w_scales[:, ci, g, :]
            else:
                codes, scales = hw_codes[:, ci - 2, g, :], hw_scales[:, ci - 2, g, :]
            nc.vector.quantize_mx(
                out=codes.bitcast(FP8X4),
                scales=scales,
                in_=grp[ci][:, g, :, :].rearrange("p n j -> p (n j)"),
            )

        def hdn_t(q, tp):
            n, g = divmod(q, 2)
            xt = ps_xt.tile([P, 2, 256], F32, name="xt")
            for u in range(2):
                for t2 in range(2):
                    a = 2 * g + u
                    nc.tensor.transpose(
                        out=xt[:, u, P * t2 : P * t2 + P],
                        in_=hr[n][:, 2 * tp + t2, :].bitcast(F32)[:, P * a : P * a + P],
                        identity=ident_f[:],
                    )
            xts[(q, tp)] = xt

        def t_out(q, tp):
            n, g = divmod(q, 2)
            if g == 0 and tp == 0:
                hg[n] = hg_pool.tile([P, 2, 2048], BF16, name="hg", align_bytes=64)
            g32 = hg[n][:, g, :].bitcast(F32)
            nc.scalar.copy(
                out=g32[:, 512 * tp : 512 * tp + 512].rearrange("p (c u) -> p c u", u=2),
                in_=xts[(q, tp)][:].rearrange("p u c -> p c u"),
            )

        def hq(q):
            n, g = divmod(q, 2)
            if g == 0:
                hc[n] = hc_pool.tile([P, 2, 512], U32, name="hc", align_bytes=64)
                hs[n] = hc_pool.tile([P, 2, 512], U8, name="hs", align_bytes=64)
            nc.vector.quantize_mx(out=hc[n][:, g, :].bitcast(FP8X4), scales=hs[n][:, g, :], in_=hg[n][:, g, :])

        def mx(k, mms):
            n, h = divmod(k, 2)
            for mm in mms:
                ps = ps_mm.tile([P, 512], F32, name="mm")
                for g in range(2):
                    nc.tensor.matmul_mx(
                        out=ps[:],
                        lhsT=w_codes[:, h, g, P * mm : P * mm + P].bitcast(FP8X4),
                        lhsT_scale=w_scales[:, h, g, P * mm : P * mm + P],
                        rhs=hc[n][:, g, :].bitcast(FP8X4),
                        rhs_scale=hs[n][:, g, :],
                        start=(g == 0),
                        stop=(g == 1),
                    )
                banks[(k, mm)] = ps

        def sq(k, mm):
            m = 4 * (k % 2) + mm
            if mm == 0:
                s4[k] = s_pool.tile([P, 4, 512], F32, name="s4")
            nc.scalar.activation(
                out=s4[k][:, mm, :], in_=banks[(k, mm)][:], func=ACT.Square, bias=bias[:, m : m + 1], scale=1.0
            )

        def stt(k, mm):
            m = 4 * (k % 2) + mm
            if mm == 0:
                c4[k] = c_pool.tile([P, 4, 512], F32, name="c4")
            nc.vector.scalar_tensor_tensor(
                out=c4[k][:, mm, :],
                in0=banks[(k, mm)][:],
                scalar=bias[:, m : m + 1],
                in1=s4[k][:, mm, :],
                op0=ALU.add,
                op1=ALU.mult,
            )

        def clamp_g(k, mm):
            nc.gpsimd.tensor_scalar(
                out=c4[k][:, mm, :], in0=c4[k][:, mm, :], scalar1=BIG, scalar2=EPS3, op0=ALU.min, op1=ALU.max
            )

        def clamp_v(k):
            both = c4[k][:, 2:4, :].rearrange("p m c -> p (m c)")
            nc.vector.tensor_scalar_max(out=both, in0=both, scalar1=EPS3)

        def sum_t(k, mms):
            n, h = divmod(k, 2)
            for mm in mms:
                for ts in range(4):
                    nc.tensor.matmul(
                        out=sums[h][:, P * mm : P * mm + P],
                        lhsT=c4[k][:, mm, P * ts : P * ts + P],
                        rhs=ident_f[:],
                        is_transpose=True,
                        start=(n == 0 and mm == 0 and ts == 0),
                        stop=(n == 8 and mm == 3 and ts == 3),
                    )

        make_identity(nc, ident_f[:])
        make_identity(nc, ident_b[:])
        nc.vector.memset(brow[:], 0.0)
        nc.vector.memset(one[:], 1.0)
        nc.scalar.dma_start(out=brow[0:8, :], in_=fc2_b.rearrange("(m p) -> m p", p=P))
        load_h(0)
        load_chunk(0)
        load_chunk(1)
        load_h(1)
        load_h(2)
        load_chunk(2)

        bt = ps_xt.tile([P, P], BF16, name="xt")
        nc.tensor.transpose(out=bt[:], in_=brow[:], identity=ident_b[:])
        nc.vector.tensor_copy(out=bias[:], in_=bt[:, 0:8])

        for q in range(2):
            for tp in range(2):
                hdn_t(q, tp)
            for tp in range(2):
                t_out(q, tp)
        load_h(3)
        hq(0)
        hq(1)
        for r in range(2):
            rg_v(r)
            rg_s(r, 0)
            rg_s(r, 1)
        cq(0)
        cq(1)

        for k in range(NSTEP):
            chunk_work = k >= 1 and 4 <= k + 3 <= 19
            mx(k, [0, 1])
            if k >= 2:
                sum_t(k - 2, [2, 3])
            if k == 0:
                hdn_t(2, 0)
                hdn_t(2, 1)
                for r in range(2, 4):
                    rg_v(r)
                    rg_s(r, 0)
                    rg_s(r, 1)
                load_chunk(3)
                load_chunk(4)
            else:
                if k + 3 < NPART:
                    hdn_t(k + 3, 0)
                if k + 2 < NPART:
                    t_out(k + 2, 1)
            sq(k, 0)
            sq(k, 1)
            if k == 0:
                t_out(2, 0)
                t_out(2, 1)
                cq(2)
                cq(3)
            else:
                clamp_v(k - 1)
            if k + 2 < NPART:
                hq(k + 2)
            if k >= 1 and 4 <= k + 2 <= 19:
                cq(k + 2)
            if chunk_work:
                rg_v(k + 3)
                rg_s(k + 3, 0)
            mx(k, [2, 3])
            if k >= 1:
                sum_t(k - 1, [0, 1])
            if k == 0:
                hdn_t(3, 0)
            elif k + 3 < NPART:
                hdn_t(k + 3, 1)
            if k + 3 < NPART:
                t_out(k + 3, 0)
            if k == 0:
                hdn_t(3, 1)
            sq(k, 2)
            sq(k, 3)
            if chunk_work:
                rg_s(k + 3, 1)
            for mm in range(4):
                stt(k, mm)
                if mm < 2:
                    clamp_g(k, mm)
            if k % 2 == 0:
                if k // 2 + 4 <= 8:
                    load_h(k // 2 + 4)
                if k >= 2 and k // 2 + 4 <= 9:
                    load_chunk(k // 2 + 4)
            if k == 12:
                nc.sync.dma_start(out=hb[:], in_=head_b.partition_broadcast(P))

        clamp_v(NSTEP - 1)
        sum_t(NSTEP - 2, [2, 3])
        nc.scalar.activation(out=lng[:, 0:512], in_=sums[0][:], func=ACT.Ln, scale=1.0 / NT)
        sum_t(NSTEP - 1, [0, 1])
        sum_t(NSTEP - 1, [2, 3])
        nc.scalar.activation(out=lng[:, 512:1024], in_=sums[1][:], func=ACT.Ln, scale=1.0 / NT)

        ps2 = {}

        def head_pass(nt, g):
            nc.tensor.matmul_mx(
                out=ps2[nt][:],
                lhsT=g_codes[:, g, :].bitcast(FP8X4),
                lhsT_scale=g_scales[:, g, :],
                rhs=hw_codes[:, nt, g, :].bitcast(FP8X4),
                rhs_scale=hw_scales[:, nt, g, :],
                start=(g == 0),
                stop=(g == 1),
            )

        lts = []
        for g in range(2):
            lt = ps_xt.tile([P, 4, P], F32, name="xt")
            for j in range(4):
                a = 4 * g + j
                nc.tensor.transpose(out=lt[:, j, :], in_=lng[:, P * a : P * a + P], identity=ident_f[:])
            lts.append(lt)
        for g in range(2):
            nc.scalar.activation(
                out=g_grp[:, g, :, :], in_=lts[g][:].rearrange("p j b -> p b j"), func=ACT.Exp, scale=1.0 / 3.0
            )
            nc.vector.quantize_mx(
                out=g_codes[:, g, :].bitcast(FP8X4),
                scales=g_scales[:, g, :],
                in_=g_grp[:, g, :, :].rearrange("p b j -> p (b j)"),
            )
            if g == 0:
                for nt in range(6):
                    if nt < 4:
                        ps2[nt] = ps_mm.tile([P, 512], F32, name="mm")
                    else:
                        ps2[nt] = ps_sum.tile([P, 512], F32, name="sum%d" % (nt - 4))
                    head_pass(nt, 0)
        nc.scalar.activation(out=dmy[:], in_=one[:], func=ACT.Abs_reciprocal_sqrt)
        for nt in range(8):
            if nt >= 6:
                ps2[nt] = ps_xt.tile([P, 512], F32, name="xt")
                head_pass(nt, 0)
            head_pass(nt, 1)
        for nt in range(8):
            cols = slice(512 * nt, 512 * nt + 512)
            nc.vector.tensor_tensor(out=d[:, cols], in0=ps2[nt][:], in1=hb[:, cols], op=ALU.add)
            nc.scalar.activation(out=junk[:], in_=d[:, cols], func=ACT.Square, accum_out=ss[:, nt : nt + 1])
        nc.scalar.activation(out=junk[:, 0:8], in_=ss[:], func=ACT.Identity, accum_out=tot[:])
        nc.scalar.activation(out=nrm[:], in_=tot[:], func=ACT.Abs_reciprocal_sqrt)
        nc.vector.tensor_scalar_min(out=rinv[:], in0=nrm[:], scalar1=1e12)
        for nt in range(8):
            cols = slice(512 * nt, 512 * nt + 512)
            if nt % 3 == 1:
                nc.scalar.activation(out=d[:, cols], in_=d[:, cols], func=ACT.Copy, scale=rinv[:, 0:1])
            else:
                nc.vector.tensor_scalar_mul(out=d[:, cols], in0=d[:, cols], scalar1=rinv[:, 0:1])
            nc.sync.dma_start(out=out[:, cols], in_=d[:, cols])
